import numpy as np
import ml_dtypes

BF16 = ml_dtypes.bfloat16


def bf(x):
    return np.asarray(x, np.float32).astype(BF16)


def f32(x):
    return np.asarray(x, np.float32)


def f64(x):
    return np.asarray(x).astype(np.float64)


def striped(idx):
    return np.tile(idx.reshape(-1, 16).T, (8, 1))


D, E, S, N, H, K = 128, 128, 1024, 2048, 512, 4


def setup_inputs():
    return {
        "var_table": f32(np.random.standard_normal((D, S))),
        "times": f32(np.random.uniform(0.0, 1.0, (1, N))),
        "values": f32(np.random.standard_normal((1, N))),
        "w1t": f32(np.random.standard_normal((E, 1))),
        "b1t": f32(0.1 * np.random.standard_normal((E, 1))),
        "w2t": bf(np.random.standard_normal((E, D)) / np.sqrt(E)),
        "w1v": f32(np.random.standard_normal((E, 1))),
        "b1v": f32(0.1 * np.random.standard_normal((E, 1))),
        "w2v": bf(np.random.standard_normal((E, D)) / np.sqrt(E)),
        "offs": striped(np.concatenate([np.random.permutation(S)[:H] for _ in range(K)])),
    }


def reference(var_table, times, values, w1t, b1t, w2t, w1v, b1v, w2v, offs):
    idx = offs[:16].T.reshape(-1)
    ht = np.tanh(f64(w1t) * f64(times) + f64(b1t))
    hv = np.tanh(f64(w1v) * f64(values) + f64(b1v))
    cve = f64(w2t).T @ ht + f64(w2v).T @ hv
    return f64(var_table)[:, idx] + cve

@@ -1,0 +1,70 @@
+import concourse.mybir as mybir
+
+F32 = mybir.dt.float32
+BF16 = mybir.dt.bfloat16
+U16 = mybir.dt.uint16
+TANH = mybir.ActivationFunctionType.Tanh
+ADD = mybir.AluOpType.add
+
+P = 128
+S = 1024
+N = 2048
+PIECE = 512
+PIECES = N // PIECE
+LIST_COLUMNS = PIECE // 16
+
+FLOPS = 2 * 2 * P * P * N
+
+
+def tile_stratsoriginal_kernel(
+    tc, var_table, times, values, w1t, b1t, w2t, w1v, b1v, w2v, offs, out
+):
+    nc = tc.nc
+    with (
+        tc.tile_pool(name="held", bufs=1) as held,
+        tc.tile_pool(name="spread", bufs=PIECES) as spread,
+        tc.tile_pool(name="hidden", bufs=2) as hidden,
+        tc.tile_pool(name="result", bufs=2) as result,
+        tc.psum_pool(name="banks", bufs=2) as banks,
+    ):
+        offsets = held.tile([P, N // 16], U16, name="offsets")
+        nc.sync.dma_start(offsets[:], offs)
+        scale_t = held.tile([P, 1], F32, name="scale_t")
+        shift_t = held.tile([P, 1], F32, name="shift_t")
+        scale_v = held.tile([P, 1], F32, name="scale_v")
+        shift_v = held.tile([P, 1], F32, name="shift_v")
+        nc.sync.dma_start(scale_t[:], w1t)
+        nc.sync.dma_start(shift_t[:], b1t)
+        nc.scalar.dma_start(scale_v[:], w1v)
+        nc.scalar.dma_start(shift_v[:], b1v)
+        mix_t = held.tile([P, P], BF16, name="mix_t")
+        mix_v = held.tile([P, P], BF16, name="mix_v")
+        table = held.tile([P, S], F32, name="table")
+        nc.gpsimd.dma_start(mix_t[:], w2t)
+        nc.gpsimd.dma_start(mix_v[:], w2v)
+        nc.gpsimd.dma_start(table[:], var_table)
+
+        for k in range(PIECES):
+            columns = slice(k * PIECE, (k + 1) * PIECE)
+
+            t_rows = spread.tile([P, PIECE], F32, name="t_rows")
+            v_rows = spread.tile([P, PIECE], F32, name="v_rows")
+            nc.sync.dma_start(t_rows[:], times[:, columns].to_broadcast([P, PIECE]))
+            nc.scalar.dma_start(v_rows[:], values[:, columns].to_broadcast([P, PIECE]))
+
+            hid_t = hidden.tile([P, PIECE], BF16, name="hid_t")
+            hid_v = hidden.tile([P, PIECE], BF16, name="hid_v")
+            nc.scalar.activation(hid_t[:], t_rows[:], TANH, bias=shift_t[:], scale=scale_t[:])
+            nc.scalar.activation(hid_v[:], v_rows[:], TANH, bias=shift_v[:], scale=scale_v[:])
+
+            bank = banks.tile([P, PIECE], F32, name="bank")
+            nc.tensor.matmul(bank[:], mix_t[:], hid_t[:], start=True, stop=False)
+            nc.tensor.matmul(bank[:], mix_v[:], hid_v[:], start=False, stop=True)
+
+            networks = result.tile([P, PIECE], F32, name="networks")
+            nc.vector.tensor_copy(networks[:], bank[:])
+
+            picked = table[:].indirect(offsets[:, k * LIST_COLUMNS : (k + 1) * LIST_COLUMNS])
+            summed = result.tile([P, PIECE], F32, name="summed")
+            nc.vector.tensor_tensor(summed[:], picked, networks[:], ADD)
+            nc.sync.dma_start(out[:, columns], summed[:])

@@ -28,34 +28,41 @@ def tile_stratsoriginal_kernel(
         tc.psum_pool(name="banks", bufs=2) as banks,
     ):
         offsets = held.tile([P, N // 16], U16, name="offsets")
-        nc.sync.dma_start(offsets[:], offs)
         scale_t = held.tile([P, 1], F32, name="scale_t")
         shift_t = held.tile([P, 1], F32, name="shift_t")
         scale_v = held.tile([P, 1], F32, name="scale_v")
         shift_v = held.tile([P, 1], F32, name="shift_v")
+        mix_t = held.tile([P, P], BF16, name="mix_t")
+        mix_v = held.tile([P, P], BF16, name="mix_v")
+        table = held.tile([P, S], F32, name="table")
+
+        t_rows = [spread.tile([P, PIECE], F32, name="t_rows") for k in range(PIECES)]
+        v_rows = [spread.tile([P, PIECE], F32, name="v_rows") for k in range(PIECES)]
         nc.sync.dma_start(scale_t[:], w1t)
         nc.sync.dma_start(shift_t[:], b1t)
         nc.scalar.dma_start(scale_v[:], w1v)
         nc.scalar.dma_start(shift_v[:], b1v)
-        mix_t = held.tile([P, P], BF16, name="mix_t")
-        mix_v = held.tile([P, P], BF16, name="mix_v")
-        table = held.tile([P, S], F32, name="table")
-        nc.gpsimd.dma_start(mix_t[:], w2t)
-        nc.gpsimd.dma_start(mix_v[:], w2v)
-        nc.gpsimd.dma_start(table[:], var_table)
+        for k in range(PIECES):
+            columns = slice(k * PIECE, (k + 1) * PIECE)
+            nc.sync.dma_start(t_rows[k][:], times[:, columns].to_broadcast([P, PIECE]))
+            nc.scalar.dma_start(v_rows[k][:], values[:, columns].to_broadcast([P, PIECE]))
+            if k == 0:
+                nc.sync.dma_start(mix_t[:], w2t)
+                nc.scalar.dma_start(mix_v[:], w2v)
+                nc.sync.dma_start(offsets[:], offs)
+                nc.sync.dma_start(table[:], var_table)
+
+        scratch = held.tile([P, 1], F32, name="scratch")
+        nc.vector.memset(scratch[:], 0.0)
+        nc.scalar.activation(scratch[:], scratch[:], TANH)
 
         for k in range(PIECES):
             columns = slice(k * PIECE, (k + 1) * PIECE)
 
-            t_rows = spread.tile([P, PIECE], F32, name="t_rows")
-            v_rows = spread.tile([P, PIECE], F32, name="v_rows")
-            nc.sync.dma_start(t_rows[:], times[:, columns].to_broadcast([P, PIECE]))
-            nc.scalar.dma_start(v_rows[:], values[:, columns].to_broadcast([P, PIECE]))
-
             hid_t = hidden.tile([P, PIECE], BF16, name="hid_t")
             hid_v = hidden.tile([P, PIECE], BF16, name="hid_v")
-            nc.scalar.activation(hid_t[:], t_rows[:], TANH, bias=shift_t[:], scale=scale_t[:])
-            nc.scalar.activation(hid_v[:], v_rows[:], TANH, bias=shift_v[:], scale=scale_v[:])
+            nc.scalar.activation(hid_t[:], t_rows[k][:], TANH, bias=shift_t[:], scale=scale_t[:])
+            nc.scalar.activation(hid_v[:], v_rows[k][:], TANH, bias=shift_v[:], scale=scale_v[:])
 
             bank = banks.tile([P, PIECE], F32, name="bank")
             nc.tensor.matmul(bank[:], mix_t[:], hid_t[:], start=True, stop=False)

@@ -4,6 +4,7 @@ F32 = mybir.dt.float32
 BF16 = mybir.dt.bfloat16
 U16 = mybir.dt.uint16
 TANH = mybir.ActivationFunctionType.Tanh
+COPY = mybir.ActivationFunctionType.Copy
 ADD = mybir.AluOpType.add
 
 P = 128
@@ -56,9 +57,7 @@ def tile_stratsoriginal_kernel(
         nc.vector.memset(scratch[:], 0.0)
         nc.scalar.activation(scratch[:], scratch[:], TANH)
 
-        for k in range(PIECES):
-            columns = slice(k * PIECE, (k + 1) * PIECE)
-
+        def networks_of(k):
             hid_t = hidden.tile([P, PIECE], BF16, name="hid_t")
             hid_v = hidden.tile([P, PIECE], BF16, name="hid_v")
             nc.scalar.activation(hid_t[:], t_rows[k][:], TANH, bias=shift_t[:], scale=scale_t[:])
@@ -67,11 +66,20 @@ def tile_stratsoriginal_kernel(
             bank = banks.tile([P, PIECE], F32, name="bank")
             nc.tensor.matmul(bank[:], mix_t[:], hid_t[:], start=True, stop=False)
             nc.tensor.matmul(bank[:], mix_v[:], hid_v[:], start=False, stop=True)
+            return bank
 
+        def finish(k, bank):
             networks = result.tile([P, PIECE], F32, name="networks")
-            nc.vector.tensor_copy(networks[:], bank[:])
+            nc.scalar.activation(networks[:], bank[:], COPY)
 
             picked = table[:].indirect(offsets[:, k * LIST_COLUMNS : (k + 1) * LIST_COLUMNS])
             summed = result.tile([P, PIECE], F32, name="summed")
             nc.vector.tensor_tensor(summed[:], picked, networks[:], ADD)
-            nc.sync.dma_start(out[:, columns], summed[:])
+            nc.sync.dma_start(out[:, k * PIECE : (k + 1) * PIECE], summed[:])
+
+        bank = networks_of(0)
+        for k in range(1, PIECES):
+            next_bank = networks_of(k)
+            finish(k - 1, bank)
+            bank = next_bank
+        finish(PIECES - 1, bank)

@@ -10,8 +10,11 @@ ADD = mybir.AluOpType.add
 P = 128
 S = 1024
 N = 2048
-PIECE = 512
+LOAD = 512
+LOADS = N // LOAD
+PIECE = 256
 PIECES = N // PIECE
+PIECES_IN_LOAD = LOAD // PIECE
 LIST_COLUMNS = PIECE // 16
 
 FLOPS = 2 * 2 * P * P * N
@@ -23,10 +26,10 @@ def tile_stratsoriginal_kernel(
     nc = tc.nc
     with (
         tc.tile_pool(name="held", bufs=1) as held,
-        tc.tile_pool(name="spread", bufs=PIECES) as spread,
-        tc.tile_pool(name="hidden", bufs=2) as hidden,
-        tc.tile_pool(name="result", bufs=2) as result,
-        tc.psum_pool(name="banks", bufs=2) as banks,
+        tc.tile_pool(name="spread", bufs=LOADS) as spread,
+        tc.tile_pool(name="hidden", bufs=4) as hidden,
+        tc.tile_pool(name="result", bufs=PIECES) as result,
+        tc.psum_pool(name="banks", bufs=4) as banks,
     ):
         offsets = held.tile([P, N // 16], U16, name="offsets")
         scale_t = held.tile([P, 1], F32, name="scale_t")
@@ -36,32 +39,42 @@ def tile_stratsoriginal_kernel(
         mix_t = held.tile([P, P], BF16, name="mix_t")
         mix_v = held.tile([P, P], BF16, name="mix_v")
         table = held.tile([P, S], F32, name="table")
+        t_rows = [spread.tile([P, LOAD], F32, name="t_rows") for g in range(LOADS)]
+        v_rows = [spread.tile([P, LOAD], F32, name="v_rows") for g in range(LOADS)]
 
-        t_rows = [spread.tile([P, PIECE], F32, name="t_rows") for k in range(PIECES)]
-        v_rows = [spread.tile([P, PIECE], F32, name="v_rows") for k in range(PIECES)]
+        def spread_load(rows, row, g):
+            nc.sync.dma_start(rows[g][:], row[:, g * LOAD : (g + 1) * LOAD].to_broadcast([P, LOAD]))
+
         nc.sync.dma_start(scale_t[:], w1t)
         nc.sync.dma_start(shift_t[:], b1t)
-        nc.scalar.dma_start(scale_v[:], w1v)
-        nc.scalar.dma_start(shift_v[:], b1v)
-        for k in range(PIECES):
-            columns = slice(k * PIECE, (k + 1) * PIECE)
-            nc.sync.dma_start(t_rows[k][:], times[:, columns].to_broadcast([P, PIECE]))
-            nc.scalar.dma_start(v_rows[k][:], values[:, columns].to_broadcast([P, PIECE]))
-            if k == 0:
-                nc.sync.dma_start(mix_t[:], w2t)
-                nc.scalar.dma_start(mix_v[:], w2v)
-                nc.sync.dma_start(offsets[:], offs)
-                nc.sync.dma_start(table[:], var_table)
+        spread_load(t_rows, times, 0)
+        nc.sync.dma_start(scale_v[:], w1v)
+        nc.sync.dma_start(shift_v[:], b1v)
+        spread_load(v_rows, values, 0)
+        nc.sync.dma_start(mix_t[:], w2t)
+        nc.sync.dma_start(table[:], var_table)
+        nc.sync.dma_start(mix_v[:], w2v)
+        nc.sync.dma_start(offsets[:], offs)
+        for g in range(1, LOADS):
+            spread_load(t_rows, times, g)
+            spread_load(v_rows, values, g)
 
         scratch = held.tile([P, 1], F32, name="scratch")
         nc.vector.memset(scratch[:], 0.0)
         nc.scalar.activation(scratch[:], scratch[:], TANH)
 
         def networks_of(k):
+            g = k // PIECES_IN_LOAD
+            columns = slice((k % PIECES_IN_LOAD) * PIECE, (k % PIECES_IN_LOAD + 1) * PIECE)
+
             hid_t = hidden.tile([P, PIECE], BF16, name="hid_t")
             hid_v = hidden.tile([P, PIECE], BF16, name="hid_v")
-            nc.scalar.activation(hid_t[:], t_rows[k][:], TANH, bias=shift_t[:], scale=scale_t[:])
-            nc.scalar.activation(hid_v[:], v_rows[k][:], TANH, bias=shift_v[:], scale=scale_v[:])
+            nc.scalar.activation(
+                hid_t[:], t_rows[g][:, columns], TANH, bias=shift_t[:], scale=scale_t[:]
+            )
+            nc.scalar.activation(
+                hid_v[:], v_rows[g][:, columns], TANH, bias=shift_v[:], scale=scale_v[:]
+            )
 
             bank = banks.tile([P, PIECE], F32, name="bank")
             nc.tensor.matmul(bank[:], mix_t[:], hid_t[:], start=True, stop=False)
@@ -70,7 +83,10 @@ def tile_stratsoriginal_kernel(
 
         def finish(k, bank):
             networks = result.tile([P, PIECE], F32, name="networks")
-            nc.scalar.activation(networks[:], bank[:], COPY)
+            if k % 2 == 0:
+                nc.scalar.activation(networks[:], bank[:], COPY)
+            else:
+                nc.vector.tensor_copy(networks[:], bank[:])
 
             picked = table[:].indirect(offsets[:, k * LIST_COLUMNS : (k + 1) * LIST_COLUMNS])
             summed = result.tile([P, PIECE], F32, name="summed")

@@ -10,7 +10,7 @@ ADD = mybir.AluOpType.add
 P = 128
 S = 1024
 N = 2048
-LOAD = 512
+LOAD = 1024
 LOADS = N // LOAD
 PIECE = 256
 PIECES = N // PIECE
@@ -27,9 +27,9 @@ def tile_stratsoriginal_kernel(
     with (
         tc.tile_pool(name="held", bufs=1) as held,
         tc.tile_pool(name="spread", bufs=LOADS) as spread,
-        tc.tile_pool(name="hidden", bufs=4) as hidden,
+        tc.tile_pool(name="hidden", bufs=PIECES) as hidden,
         tc.tile_pool(name="result", bufs=PIECES) as result,
-        tc.psum_pool(name="banks", bufs=4) as banks,
+        tc.psum_pool(name="banks", bufs=PIECES) as banks,
     ):
         offsets = held.tile([P, N // 16], U16, name="offsets")
         scale_t = held.tile([P, 1], F32, name="scale_t")
@@ -47,9 +47,9 @@ def tile_stratsoriginal_kernel(
 
         nc.sync.dma_start(scale_t[:], w1t)
         nc.sync.dma_start(shift_t[:], b1t)
-        spread_load(t_rows, times, 0)
         nc.sync.dma_start(scale_v[:], w1v)
         nc.sync.dma_start(shift_v[:], b1v)
+        spread_load(t_rows, times, 0)
         spread_load(v_rows, values, 0)
         nc.sync.dma_start(mix_t[:], w2t)
         nc.sync.dma_start(table[:], var_table)
@@ -63,23 +63,24 @@ def tile_stratsoriginal_kernel(
         nc.vector.memset(scratch[:], 0.0)
         nc.scalar.activation(scratch[:], scratch[:], TANH)
 
-        def networks_of(k):
-            g = k // PIECES_IN_LOAD
-            columns = slice((k % PIECES_IN_LOAD) * PIECE, (k % PIECES_IN_LOAD + 1) * PIECE)
+        def columns_of(k):
+            return slice((k % PIECES_IN_LOAD) * PIECE, (k % PIECES_IN_LOAD + 1) * PIECE)
 
+        def time_network(k, g):
             hid_t = hidden.tile([P, PIECE], BF16, name="hid_t")
-            hid_v = hidden.tile([P, PIECE], BF16, name="hid_v")
             nc.scalar.activation(
-                hid_t[:], t_rows[g][:, columns], TANH, bias=shift_t[:], scale=scale_t[:]
+                hid_t[:], t_rows[g][:, columns_of(k)], TANH, bias=shift_t[:], scale=scale_t[:]
             )
-            nc.scalar.activation(
-                hid_v[:], v_rows[g][:, columns], TANH, bias=shift_v[:], scale=scale_v[:]
-            )
-
             bank = banks.tile([P, PIECE], F32, name="bank")
             nc.tensor.matmul(bank[:], mix_t[:], hid_t[:], start=True, stop=False)
-            nc.tensor.matmul(bank[:], mix_v[:], hid_v[:], start=False, stop=True)
             return bank
+
+        def value_network(k, g, bank):
+            hid_v = hidden.tile([P, PIECE], BF16, name="hid_v")
+            nc.scalar.activation(
+                hid_v[:], v_rows[g][:, columns_of(k)], TANH, bias=shift_v[:], scale=scale_v[:]
+            )
+            nc.tensor.matmul(bank[:], mix_v[:], hid_v[:], start=False, stop=True)
 
         def finish(k, bank):
             networks = result.tile([P, PIECE], F32, name="networks")
@@ -93,9 +94,13 @@ def tile_stratsoriginal_kernel(
             nc.vector.tensor_tensor(summed[:], picked, networks[:], ADD)
             nc.sync.dma_start(out[:, k * PIECE : (k + 1) * PIECE], summed[:])
 
-        bank = networks_of(0)
-        for k in range(1, PIECES):
-            next_bank = networks_of(k)
-            finish(k - 1, bank)
-            bank = next_bank
-        finish(PIECES - 1, bank)
+        bank_of = {}
+        for g in range(LOADS):
+            pieces = range(g * PIECES_IN_LOAD, (g + 1) * PIECES_IN_LOAD)
+            for k in pieces:
+                bank_of[k] = time_network(k, g)
+            for k in pieces:
+                value_network(k, g, bank_of[k])
+                if k > 0:
+                    finish(k - 1, bank_of[k - 1])
+        finish(PIECES - 1, bank_of[PIECES - 1])

@@ -10,12 +10,11 @@ ADD = mybir.AluOpType.add
 P = 128
 S = 1024
 N = 2048
-LOAD = 1024
-LOADS = N // LOAD
 PIECE = 256
 PIECES = N // PIECE
-PIECES_IN_LOAD = LOAD // PIECE
 LIST_COLUMNS = PIECE // 16
+LOAD_WIDTHS = (N // 4, N // 4, N // 2)
+SHORT_LOADS = 2
 
 FLOPS = 2 * 2 * P * P * N
 
@@ -26,7 +25,6 @@ def tile_stratsoriginal_kernel(
     nc = tc.nc
     with (
         tc.tile_pool(name="held", bufs=1) as held,
-        tc.tile_pool(name="spread", bufs=LOADS) as spread,
         tc.tile_pool(name="hidden", bufs=PIECES) as hidden,
         tc.tile_pool(name="result", bufs=PIECES) as result,
         tc.psum_pool(name="banks", bufs=PIECES) as banks,
@@ -39,37 +37,40 @@ def tile_stratsoriginal_kernel(
         mix_t = held.tile([P, P], BF16, name="mix_t")
         mix_v = held.tile([P, P], BF16, name="mix_v")
         table = held.tile([P, S], F32, name="table")
-        t_rows = [spread.tile([P, LOAD], F32, name="t_rows") for g in range(LOADS)]
-        v_rows = [spread.tile([P, LOAD], F32, name="v_rows") for g in range(LOADS)]
+        t_rows = [held.tile([P, w], F32, name=f"t_rows{g}") for g, w in enumerate(LOAD_WIDTHS)]
+        v_rows = [held.tile([P, w], F32, name=f"v_rows{g}") for g, w in enumerate(LOAD_WIDTHS)]
+        load_starts = [sum(LOAD_WIDTHS[:g]) for g in range(len(LOAD_WIDTHS))]
 
-        def spread_load(rows, row, g):
-            nc.sync.dma_start(rows[g][:], row[:, g * LOAD : (g + 1) * LOAD].to_broadcast([P, LOAD]))
+        def spread_load(queue, rows, row, g):
+            run = row[:, load_starts[g] : load_starts[g] + LOAD_WIDTHS[g]]
+            queue.dma_start(rows[g][:], run.to_broadcast([P, LOAD_WIDTHS[g]]))
 
         nc.sync.dma_start(scale_t[:], w1t)
+        nc.scalar.dma_start(scale_v[:], w1v)
         nc.sync.dma_start(shift_t[:], b1t)
-        nc.sync.dma_start(scale_v[:], w1v)
-        nc.sync.dma_start(shift_v[:], b1v)
-        spread_load(t_rows, times, 0)
-        spread_load(v_rows, values, 0)
+        nc.scalar.dma_start(shift_v[:], b1v)
+        for g in range(SHORT_LOADS):
+            spread_load(nc.sync, t_rows, times, g)
+            spread_load(nc.scalar, v_rows, values, g)
         nc.sync.dma_start(mix_t[:], w2t)
-        nc.sync.dma_start(table[:], var_table)
         nc.sync.dma_start(mix_v[:], w2v)
         nc.sync.dma_start(offsets[:], offs)
-        for g in range(1, LOADS):
-            spread_load(t_rows, times, g)
-            spread_load(v_rows, values, g)
+        nc.sync.dma_start(table[:], var_table)
+        for g in range(SHORT_LOADS, len(LOAD_WIDTHS)):
+            spread_load(nc.sync, t_rows, times, g)
+            spread_load(nc.sync, v_rows, values, g)
 
         scratch = held.tile([P, 1], F32, name="scratch")
         nc.vector.memset(scratch[:], 0.0)
         nc.scalar.activation(scratch[:], scratch[:], TANH)
 
-        def columns_of(k):
-            return slice((k % PIECES_IN_LOAD) * PIECE, (k % PIECES_IN_LOAD + 1) * PIECE)
+        def columns_of(k, g):
+            return slice(k * PIECE - load_starts[g], (k + 1) * PIECE - load_starts[g])
 
         def time_network(k, g):
             hid_t = hidden.tile([P, PIECE], BF16, name="hid_t")
             nc.scalar.activation(
-                hid_t[:], t_rows[g][:, columns_of(k)], TANH, bias=shift_t[:], scale=scale_t[:]
+                hid_t[:], t_rows[g][:, columns_of(k, g)], TANH, bias=shift_t[:], scale=scale_t[:]
             )
             bank = banks.tile([P, PIECE], F32, name="bank")
             nc.tensor.matmul(bank[:], mix_t[:], hid_t[:], start=True, stop=False)
@@ -78,29 +79,28 @@ def tile_stratsoriginal_kernel(
         def value_network(k, g, bank):
             hid_v = hidden.tile([P, PIECE], BF16, name="hid_v")
             nc.scalar.activation(
-                hid_v[:], v_rows[g][:, columns_of(k)], TANH, bias=shift_v[:], scale=scale_v[:]
+                hid_v[:], v_rows[g][:, columns_of(k, g)], TANH, bias=shift_v[:], scale=scale_v[:]
             )
             nc.tensor.matmul(bank[:], mix_v[:], hid_v[:], start=False, stop=True)
 
-        def finish(k, bank):
+        def finish(k, g, bank):
             networks = result.tile([P, PIECE], F32, name="networks")
-            if k % 2 == 0:
-                nc.scalar.activation(networks[:], bank[:], COPY)
-            else:
+            if g < SHORT_LOADS:
                 nc.vector.tensor_copy(networks[:], bank[:])
+            else:
+                nc.scalar.activation(networks[:], bank[:], COPY)
 
             picked = table[:].indirect(offsets[:, k * LIST_COLUMNS : (k + 1) * LIST_COLUMNS])
             summed = result.tile([P, PIECE], F32, name="summed")
             nc.vector.tensor_tensor(summed[:], picked, networks[:], ADD)
             nc.sync.dma_start(out[:, k * PIECE : (k + 1) * PIECE], summed[:])
 
-        bank_of = {}
-        for g in range(LOADS):
-            pieces = range(g * PIECES_IN_LOAD, (g + 1) * PIECES_IN_LOAD)
-            for k in pieces:
-                bank_of[k] = time_network(k, g)
-            for k in pieces:
+        for g in range(len(LOAD_WIDTHS)):
+            first = load_starts[g] // PIECE
+            last = first + LOAD_WIDTHS[g] // PIECE - 1
+            bank_of = {k: time_network(k, g) for k in range(first, last + 1)}
+            for k in range(first, last + 1):
                 value_network(k, g, bank_of[k])
-                if k > 0:
-                    finish(k - 1, bank_of[k - 1])
-        finish(PIECES - 1, bank_of[PIECES - 1])
+                if k > first:
+                    finish(k - 1, g, bank_of[k - 1])
+            finish(last, g, bank_of[last])

@@ -10,11 +10,14 @@ ADD = mybir.AluOpType.add
 P = 128
 S = 1024
 N = 2048
+LOAD = 1024
+LOADS = N // LOAD
 PIECE = 256
 PIECES = N // PIECE
+PIECES_IN_LOAD = LOAD // PIECE
+PIECES_IN_STORE = 2
+STORE = PIECES_IN_STORE * PIECE
 LIST_COLUMNS = PIECE // 16
-LOAD_WIDTHS = (N // 4, N // 4, N // 2)
-SHORT_LOADS = 2
 
 FLOPS = 2 * 2 * P * P * N
 
@@ -25,8 +28,10 @@ def tile_stratsoriginal_kernel(
     nc = tc.nc
     with (
         tc.tile_pool(name="held", bufs=1) as held,
+        tc.tile_pool(name="spread", bufs=LOADS) as spread,
         tc.tile_pool(name="hidden", bufs=PIECES) as hidden,
         tc.tile_pool(name="result", bufs=PIECES) as result,
+        tc.tile_pool(name="stored", bufs=N // STORE) as stored,
         tc.psum_pool(name="banks", bufs=PIECES) as banks,
     ):
         offsets = held.tile([P, N // 16], U16, name="offsets")
@@ -37,40 +42,37 @@ def tile_stratsoriginal_kernel(
         mix_t = held.tile([P, P], BF16, name="mix_t")
         mix_v = held.tile([P, P], BF16, name="mix_v")
         table = held.tile([P, S], F32, name="table")
-        t_rows = [held.tile([P, w], F32, name=f"t_rows{g}") for g, w in enumerate(LOAD_WIDTHS)]
-        v_rows = [held.tile([P, w], F32, name=f"v_rows{g}") for g, w in enumerate(LOAD_WIDTHS)]
-        load_starts = [sum(LOAD_WIDTHS[:g]) for g in range(len(LOAD_WIDTHS))]
+        t_rows = [spread.tile([P, LOAD], F32, name="t_rows") for g in range(LOADS)]
+        v_rows = [spread.tile([P, LOAD], F32, name="v_rows") for g in range(LOADS)]
 
-        def spread_load(queue, rows, row, g):
-            run = row[:, load_starts[g] : load_starts[g] + LOAD_WIDTHS[g]]
-            queue.dma_start(rows[g][:], run.to_broadcast([P, LOAD_WIDTHS[g]]))
+        def spread_load(rows, row, g):
+            nc.sync.dma_start(rows[g][:], row[:, g * LOAD : (g + 1) * LOAD].to_broadcast([P, LOAD]))
 
         nc.sync.dma_start(scale_t[:], w1t)
-        nc.scalar.dma_start(scale_v[:], w1v)
         nc.sync.dma_start(shift_t[:], b1t)
-        nc.scalar.dma_start(shift_v[:], b1v)
-        for g in range(SHORT_LOADS):
-            spread_load(nc.sync, t_rows, times, g)
-            spread_load(nc.scalar, v_rows, values, g)
+        nc.sync.dma_start(scale_v[:], w1v)
+        nc.sync.dma_start(shift_v[:], b1v)
+        spread_load(t_rows, times, 0)
+        spread_load(v_rows, values, 0)
         nc.sync.dma_start(mix_t[:], w2t)
+        nc.sync.dma_start(table[:], var_table)
         nc.sync.dma_start(mix_v[:], w2v)
         nc.sync.dma_start(offsets[:], offs)
-        nc.sync.dma_start(table[:], var_table)
-        for g in range(SHORT_LOADS, len(LOAD_WIDTHS)):
-            spread_load(nc.sync, t_rows, times, g)
-            spread_load(nc.sync, v_rows, values, g)
+        for g in range(1, LOADS):
+            spread_load(t_rows, times, g)
+            spread_load(v_rows, values, g)
 
         scratch = held.tile([P, 1], F32, name="scratch")
         nc.vector.memset(scratch[:], 0.0)
         nc.scalar.activation(scratch[:], scratch[:], TANH)
 
-        def columns_of(k, g):
-            return slice(k * PIECE - load_starts[g], (k + 1) * PIECE - load_starts[g])
+        def columns_of(k):
+            return slice((k % PIECES_IN_LOAD) * PIECE, (k % PIECES_IN_LOAD + 1) * PIECE)
 
         def time_network(k, g):
             hid_t = hidden.tile([P, PIECE], BF16, name="hid_t")
             nc.scalar.activation(
-                hid_t[:], t_rows[g][:, columns_of(k, g)], TANH, bias=shift_t[:], scale=scale_t[:]
+                hid_t[:], t_rows[g][:, columns_of(k)], TANH, bias=shift_t[:], scale=scale_t[:]
             )
             bank = banks.tile([P, PIECE], F32, name="bank")
             nc.tensor.matmul(bank[:], mix_t[:], hid_t[:], start=True, stop=False)
@@ -79,28 +81,33 @@ def tile_stratsoriginal_kernel(
         def value_network(k, g, bank):
             hid_v = hidden.tile([P, PIECE], BF16, name="hid_v")
             nc.scalar.activation(
-                hid_v[:], v_rows[g][:, columns_of(k, g)], TANH, bias=shift_v[:], scale=scale_v[:]
+                hid_v[:], v_rows[g][:, columns_of(k)], TANH, bias=shift_v[:], scale=scale_v[:]
             )
             nc.tensor.matmul(bank[:], mix_v[:], hid_v[:], start=False, stop=True)
 
-        def finish(k, g, bank):
+        summed_of = {}
+
+        def finish(k, bank):
             networks = result.tile([P, PIECE], F32, name="networks")
-            if g < SHORT_LOADS:
-                nc.vector.tensor_copy(networks[:], bank[:])
-            else:
-                nc.scalar.activation(networks[:], bank[:], COPY)
+            nc.scalar.activation(networks[:], bank[:], COPY)
 
             picked = table[:].indirect(offsets[:, k * LIST_COLUMNS : (k + 1) * LIST_COLUMNS])
-            summed = result.tile([P, PIECE], F32, name="summed")
-            nc.vector.tensor_tensor(summed[:], picked, networks[:], ADD)
-            nc.sync.dma_start(out[:, k * PIECE : (k + 1) * PIECE], summed[:])
+            place = k % PIECES_IN_STORE
+            if place == 0:
+                summed_of[k // PIECES_IN_STORE] = stored.tile([P, STORE], F32, name="summed")
+            summed = summed_of[k // PIECES_IN_STORE]
+            nc.vector.tensor_tensor(
+                summed[:, place * PIECE : (place + 1) * PIECE], picked, networks[:], ADD
+            )
+            if place == PIECES_IN_STORE - 1:
+                nc.sync.dma_start(out[:, (k + 1) * PIECE - STORE : (k + 1) * PIECE], summed[:])
 
-        for g in range(len(LOAD_WIDTHS)):
-            first = load_starts[g] // PIECE
-            last = first + LOAD_WIDTHS[g] // PIECE - 1
+        for g in range(LOADS):
+            first = g * PIECES_IN_LOAD
+            last = first + PIECES_IN_LOAD - 1
             bank_of = {k: time_network(k, g) for k in range(first, last + 1)}
             for k in range(first, last + 1):
                 value_network(k, g, bank_of[k])
                 if k > first:
-                    finish(k - 1, g, bank_of[k - 1])
-            finish(last, g, bank_of[last])
+                    finish(k - 1, bank_of[k - 1])
+            finish(last, bank_of[last])

@@ -45,13 +45,14 @@ def tile_stratsoriginal_kernel(
         t_rows = [spread.tile([P, LOAD], F32, name="t_rows") for g in range(LOADS)]
         v_rows = [spread.tile([P, LOAD], F32, name="v_rows") for g in range(LOADS)]
 
-        def spread_load(rows, row, g):
-            nc.sync.dma_start(rows[g][:], row[:, g * LOAD : (g + 1) * LOAD].to_broadcast([P, LOAD]))
+        def spread_load(tiles, source, g):
+            run = source[:, g * LOAD : (g + 1) * LOAD]
+            nc.sync.dma_start(tiles[g][:], run.to_broadcast([P, LOAD]))
 
         nc.sync.dma_start(scale_t[:], w1t)
+        nc.scalar.dma_start(scale_v[:], w1v)
         nc.sync.dma_start(shift_t[:], b1t)
-        nc.sync.dma_start(scale_v[:], w1v)
-        nc.sync.dma_start(shift_v[:], b1v)
+        nc.scalar.dma_start(shift_v[:], b1v)
         spread_load(t_rows, times, 0)
         spread_load(v_rows, values, 0)
         nc.sync.dma_start(mix_t[:], w2t)

@@ -6,15 +6,19 @@ U16 = mybir.dt.uint16
 TANH = mybir.ActivationFunctionType.Tanh
 COPY = mybir.ActivationFunctionType.Copy
 ADD = mybir.AluOpType.add
+SUBTRACT = mybir.AluOpType.subtract
+NOT_EQUAL = mybir.AluOpType.not_equal
 
 P = 128
 S = 1024
 N = 2048
-LOAD = 1024
-LOADS = N // LOAD
+ROW = 128
+ROWS_EACH = N // ROW
+ROWS = 2 * ROWS_EACH
+PARTS = 3
 PIECE = 256
 PIECES = N // PIECE
-PIECES_IN_LOAD = LOAD // PIECE
+ROWS_IN_PIECE = PIECE // ROW
 PIECES_IN_STORE = 2
 STORE = PIECES_IN_STORE * PIECE
 LIST_COLUMNS = PIECE // 16
@@ -28,11 +32,11 @@ def tile_stratsoriginal_kernel(
     nc = tc.nc
     with (
         tc.tile_pool(name="held", bufs=1) as held,
-        tc.tile_pool(name="spread", bufs=LOADS) as spread,
         tc.tile_pool(name="hidden", bufs=PIECES) as hidden,
         tc.tile_pool(name="result", bufs=PIECES) as result,
         tc.tile_pool(name="stored", bufs=N // STORE) as stored,
-        tc.psum_pool(name="banks", bufs=PIECES) as banks,
+        tc.psum_pool(name="spread", bufs=4) as spread,
+        tc.psum_pool(name="banks", bufs=4) as banks,
     ):
         offsets = held.tile([P, N // 16], U16, name="offsets")
         scale_t = held.tile([P, 1], F32, name="scale_t")
@@ -42,55 +46,86 @@ def tile_stratsoriginal_kernel(
         mix_t = held.tile([P, P], BF16, name="mix_t")
         mix_v = held.tile([P, P], BF16, name="mix_v")
         table = held.tile([P, S], F32, name="table")
-        t_rows = [spread.tile([P, LOAD], F32, name="t_rows") for g in range(LOADS)]
-        v_rows = [spread.tile([P, LOAD], F32, name="v_rows") for g in range(LOADS)]
+        numbers = held.tile([PARTS * ROWS, ROW], F32, name="numbers")
+        rest = held.tile([2 * ROWS, ROW], F32, name="rest")
+        parts = held.tile([P, ROW], BF16, name="parts")
+        pick = held.tile([P, ROWS], BF16, name="pick")
 
-        def spread_load(tiles, source, g):
-            run = source[:, g * LOAD : (g + 1) * LOAD]
-            nc.sync.dma_start(tiles[g][:], run.to_broadcast([P, LOAD]))
-
-        nc.sync.dma_start(scale_t[:], w1t)
-        nc.scalar.dma_start(scale_v[:], w1v)
-        nc.sync.dma_start(shift_t[:], b1t)
-        nc.scalar.dma_start(shift_v[:], b1v)
-        spread_load(t_rows, times, 0)
-        spread_load(v_rows, values, 0)
-        nc.sync.dma_start(mix_t[:], w2t)
+        for part in range(PARTS):
+            first = part * ROWS
+            nc.sync.dma_start(
+                numbers[first : first + ROWS_EACH, :],
+                times.rearrange("o (r c) -> (o r) c", c=ROW),
+            )
+            nc.sync.dma_start(
+                numbers[first + ROWS_EACH : first + ROWS, :],
+                values.rearrange("o (r c) -> (o r) c", c=ROW),
+            )
         nc.sync.dma_start(table[:], var_table)
-        nc.sync.dma_start(mix_v[:], w2v)
         nc.sync.dma_start(offsets[:], offs)
-        for g in range(1, LOADS):
-            spread_load(t_rows, times, g)
-            spread_load(v_rows, values, g)
+        nc.sync.dma_start(scale_t[:], w1t)
+        nc.sync.dma_start(shift_t[:], b1t)
+        nc.sync.dma_start(scale_v[:], w1v)
+        nc.sync.dma_start(shift_v[:], b1v)
+        nc.sync.dma_start(mix_t[:], w2t)
+        nc.sync.dma_start(mix_v[:], w2v)
 
         scratch = held.tile([P, 1], F32, name="scratch")
         nc.vector.memset(scratch[:], 0.0)
         nc.scalar.activation(scratch[:], scratch[:], TANH)
 
-        def columns_of(k):
-            return slice((k % PIECES_IN_LOAD) * PIECE, (k % PIECES_IN_LOAD + 1) * PIECE)
+        nc.gpsimd.memset(pick[:], 0.0)
+        for part in range(PARTS):
+            nc.gpsimd.affine_select(
+                out=pick[:],
+                in_=pick[:],
+                compare_op=NOT_EQUAL,
+                fill=1.0,
+                base=-part * ROWS,
+                pattern=[[-1, ROWS]],
+                channel_multiplier=1,
+            )
 
-        def time_network(k, g):
+        nc.vector.memset(parts[PARTS * ROWS :, :], 0.0)
+        nc.vector.tensor_copy(parts[: 3 * ROWS, :], numbers[:])
+        nc.vector.tensor_tensor(rest[:], numbers[: 2 * ROWS, :], parts[: 2 * ROWS, :], SUBTRACT)
+        nc.vector.tensor_copy(parts[: 2 * ROWS, :], rest[:])
+        nc.vector.tensor_tensor(parts[:ROWS, :], rest[:ROWS, :], parts[:ROWS, :], SUBTRACT)
+
+        def spread_piece(k):
+            bank = spread.tile([P, 2 * PIECE], F32, name="everywhere")
+            for half in range(2):
+                for i in range(ROWS_IN_PIECE):
+                    r = half * ROWS_EACH + k * ROWS_IN_PIECE + i
+                    place = half * PIECE + i * ROW
+                    nc.tensor.matmul(
+                        bank[:, place : place + ROW],
+                        pick[:, r : r + 1].to_broadcast([P, P]),
+                        parts[:],
+                        start=True,
+                        stop=True,
+                    )
+            return bank
+
+        def networks(k, everywhere):
             hid_t = hidden.tile([P, PIECE], BF16, name="hid_t")
             nc.scalar.activation(
-                hid_t[:], t_rows[g][:, columns_of(k)], TANH, bias=shift_t[:], scale=scale_t[:]
+                hid_t[:], everywhere[:, :PIECE], TANH, bias=shift_t[:], scale=scale_t[:]
+            )
+            hid_v = hidden.tile([P, PIECE], BF16, name="hid_v")
+            nc.scalar.activation(
+                hid_v[:], everywhere[:, PIECE:], TANH, bias=shift_v[:], scale=scale_v[:]
             )
             bank = banks.tile([P, PIECE], F32, name="bank")
             nc.tensor.matmul(bank[:], mix_t[:], hid_t[:], start=True, stop=False)
-            return bank
-
-        def value_network(k, g, bank):
-            hid_v = hidden.tile([P, PIECE], BF16, name="hid_v")
-            nc.scalar.activation(
-                hid_v[:], v_rows[g][:, columns_of(k)], TANH, bias=shift_v[:], scale=scale_v[:]
-            )
             nc.tensor.matmul(bank[:], mix_v[:], hid_v[:], start=False, stop=True)
+            return bank
 
         summed_of = {}
 
         def finish(k, bank):
-            networks = result.tile([P, PIECE], F32, name="networks")
-            nc.scalar.activation(networks[:], bank[:], COPY)
+            both = result.tile([P, PIECE], F32, name="both")
+            nc.scalar.activation(both[:], bank[:], COPY)
 
             picked = table[:].indirect(offsets[:, k * LIST_COLUMNS : (k + 1) * LIST_COLUMNS])
             place = k % PIECES_IN_STORE
@@ -98,17 +133,17 @@ def tile_stratsoriginal_kernel(
                 summed_of[k // PIECES_IN_STORE] = stored.tile([P, STORE], F32, name="summed")
             summed = summed_of[k // PIECES_IN_STORE]
             nc.vector.tensor_tensor(
-                summed[:, place * PIECE : (place + 1) * PIECE], picked, networks[:], ADD
+                summed[:, place * PIECE : (place + 1) * PIECE], picked, both[:], ADD
             )
             if place == PIECES_IN_STORE - 1:
                 nc.sync.dma_start(out[:, (k + 1) * PIECE - STORE : (k + 1) * PIECE], summed[:])
 
-        for g in range(LOADS):
-            first = g * PIECES_IN_LOAD
-            last = first + PIECES_IN_LOAD - 1
-            bank_of = {k: time_network(k, g) for k in range(first, last + 1)}
-            for k in range(first, last + 1):
-                value_network(k, g, bank_of[k])
-                if k > first:
-                    finish(k - 1, bank_of[k - 1])
-            finish(last, bank_of[last])
+        everywhere_of = {0: spread_piece(0)}
+        bank_of = {}
+        for k in range(PIECES):
+            if k + 1 < PIECES:
+                everywhere_of[k + 1] = spread_piece(k + 1)
+            bank_of[k] = networks(k, everywhere_of[k])
+            if k > 0:
+                finish(k - 1, bank_of[k - 1])
+        finish(PIECES - 1, bank_of[PIECES - 1])

@@ -46,29 +46,27 @@ def tile_stratsoriginal_kernel(
         mix_t = held.tile([P, P], BF16, name="mix_t")
         mix_v = held.tile([P, P], BF16, name="mix_v")
         table = held.tile([P, S], F32, name="table")
-        numbers = held.tile([PARTS * ROWS, ROW], F32, name="numbers")
-        rest = held.tile([2 * ROWS, ROW], F32, name="rest")
-        parts = held.tile([P, ROW], BF16, name="parts")
+        words = held.tile([P, ROW], F32, name="words")
         pick = held.tile([P, ROWS], BF16, name="pick")
 
         for part in range(PARTS):
             first = part * ROWS
             nc.sync.dma_start(
-                numbers[first : first + ROWS_EACH, :],
+                words[first : first + ROWS_EACH, :],
                 times.rearrange("o (r c) -> (o r) c", c=ROW),
             )
             nc.sync.dma_start(
-                numbers[first + ROWS_EACH : first + ROWS, :],
+                words[first + ROWS_EACH : first + ROWS, :],
                 values.rearrange("o (r c) -> (o r) c", c=ROW),
             )
-        nc.sync.dma_start(table[:], var_table)
-        nc.sync.dma_start(offsets[:], offs)
         nc.sync.dma_start(scale_t[:], w1t)
         nc.sync.dma_start(shift_t[:], b1t)
         nc.sync.dma_start(scale_v[:], w1v)
         nc.sync.dma_start(shift_v[:], b1v)
         nc.sync.dma_start(mix_t[:], w2t)
         nc.sync.dma_start(mix_v[:], w2v)
+        nc.sync.dma_start(table[:], var_table)
+        nc.sync.dma_start(offsets[:], offs)
 
         scratch = held.tile([P, 1], F32, name="scratch")
         nc.vector.memset(scratch[:], 0.0)
@@ -86,11 +84,12 @@ def tile_stratsoriginal_kernel(
                 channel_multiplier=1,
             )
 
-        nc.vector.memset(parts[PARTS * ROWS :, :], 0.0)
-        nc.vector.tensor_copy(parts[: 3 * ROWS, :], numbers[:])
-        nc.vector.tensor_tensor(rest[:], numbers[: 2 * ROWS, :], parts[: 2 * ROWS, :], SUBTRACT)
-        nc.vector.tensor_copy(parts[: 2 * ROWS, :], rest[:])
-        nc.vector.tensor_tensor(parts[:ROWS, :], rest[:ROWS, :], parts[:ROWS, :], SUBTRACT)
+        def upper(rows):
+            return words[:rows, :].bitcast(BF16)[:, 1::2]
+
+        nc.vector.memset(words[PARTS * ROWS :, :], 0.0)
+        nc.vector.tensor_tensor(words[: 2 * ROWS, :], words[: 2 * ROWS, :], upper(2 * ROWS), SUBTRACT)
+        nc.vector.tensor_tensor(words[:ROWS, :], words[:ROWS, :], upper(ROWS), SUBTRACT)
 
         def spread_piece(k):
             bank = spread.tile([P, 2 * PIECE], F32, name="everywhere")
@@ -101,7 +100,7 @@ def tile_stratsoriginal_kernel(
                     nc.tensor.matmul(
                         bank[:, place : place + ROW],
                         pick[:, r : r + 1].to_broadcast([P, P]),
-                        parts[:],
+                        upper(P),
                         start=True,
                         stop=True,
                     )

@@ -19,8 +19,6 @@ PARTS = 3
 PIECE = 256
 PIECES = N // PIECE
 ROWS_IN_PIECE = PIECE // ROW
-PIECES_IN_STORE = 2
-STORE = PIECES_IN_STORE * PIECE
 LIST_COLUMNS = PIECE // 16
 
 FLOPS = 2 * 2 * P * P * N
@@ -32,9 +30,9 @@ def tile_stratsoriginal_kernel(
     nc = tc.nc
     with (
         tc.tile_pool(name="held", bufs=1) as held,
-        tc.tile_pool(name="hidden", bufs=PIECES) as hidden,
+        tc.tile_pool(name="hidden", bufs=2 * PIECES) as hidden,
         tc.tile_pool(name="result", bufs=PIECES) as result,
-        tc.tile_pool(name="stored", bufs=N // STORE) as stored,
+        tc.tile_pool(name="stored", bufs=PIECES) as stored,
         tc.psum_pool(name="spread", bufs=4) as spread,
         tc.psum_pool(name="banks", bufs=4) as banks,
     ):
@@ -91,58 +89,37 @@ def tile_stratsoriginal_kernel(
         nc.vector.tensor_tensor(words[: 2 * ROWS, :], words[: 2 * ROWS, :], upper(2 * ROWS), SUBTRACT)
         nc.vector.tensor_tensor(words[:ROWS, :], words[:ROWS, :], upper(ROWS), SUBTRACT)
 
-        def spread_piece(k):
-            bank = spread.tile([P, 2 * PIECE], F32, name="everywhere")
-            for half in range(2):
-                for i in range(ROWS_IN_PIECE):
-                    r = half * ROWS_EACH + k * ROWS_IN_PIECE + i
-                    place = half * PIECE + i * ROW
-                    nc.tensor.matmul(
-                        bank[:, place : place + ROW],
-                        pick[:, r : r + 1].to_broadcast([P, P]),
-                        upper(P),
-                        start=True,
-                        stop=True,
-                    )
-            return bank
+        def hidden_layer(k, first_row, scale, shift):
+            everywhere = spread.tile([P, PIECE], F32, name="everywhere")
+            for i in range(ROWS_IN_PIECE):
+                r = first_row + k * ROWS_IN_PIECE + i
+                nc.tensor.matmul(
+                    everywhere[:, i * ROW : (i + 1) * ROW],
+                    pick[:, r : r + 1].to_broadcast([P, P]),
+                    upper(P),
+                    start=True,
+                    stop=True,
+                )
+            hid = hidden.tile([P, PIECE], BF16, name="hid")
+            nc.scalar.activation(hid[:], everywhere[:], TANH, bias=shift[:], scale=scale[:])
+            return hid
 
-        def networks(k, everywhere):
-            hid_t = hidden.tile([P, PIECE], BF16, name="hid_t")
-            nc.scalar.activation(
-                hid_t[:], everywhere[:, :PIECE], TANH, bias=shift_t[:], scale=scale_t[:]
-            )
-            hid_v = hidden.tile([P, PIECE], BF16, name="hid_v")
-            nc.scalar.activation(
-                hid_v[:], everywhere[:, PIECE:], TANH, bias=shift_v[:], scale=scale_v[:]
-            )
+        def mix(hid_t, hid_v):
             bank = banks.tile([P, PIECE], F32, name="bank")
             nc.tensor.matmul(bank[:], mix_t[:], hid_t[:], start=True, stop=False)
             nc.tensor.matmul(bank[:], mix_v[:], hid_v[:], start=False, stop=True)
             return bank
-
-        summed_of = {}
 
         def finish(k, bank):
             both = result.tile([P, PIECE], F32, name="both")
             nc.scalar.activation(both[:], bank[:], COPY)
 
             picked = table[:].indirect(offsets[:, k * LIST_COLUMNS : (k + 1) * LIST_COLUMNS])
-            place = k % PIECES_IN_STORE
-            if place == 0:
-                summed_of[k // PIECES_IN_STORE] = stored.tile([P, STORE], F32, name="summed")
-            summed = summed_of[k // PIECES_IN_STORE]
-            nc.vector.tensor_tensor(
-                summed[:, place * PIECE : (place + 1) * PIECE], picked, both[:], ADD
-            )
-            if place == PIECES_IN_STORE - 1:
-                nc.sync.dma_start(out[:, (k + 1) * PIECE - STORE : (k + 1) * PIECE], summed[:])
+            summed = stored.tile([P, PIECE], F32, name="summed")
+            nc.vector.tensor_tensor(summed[:], picked, both[:], ADD)
+            nc.sync.dma_start(out[:, k * PIECE : (k + 1) * PIECE], summed[:])
 
-        everywhere_of = {0: spread_piece(0)}
-        bank_of = {}
         for k in range(PIECES):
-            if k + 1 < PIECES:
-                everywhere_of[k + 1] = spread_piece(k + 1)
-            bank_of[k] = networks(k, everywhere_of[k])
-            if k > 0:
-                finish(k - 1, bank_of[k - 1])
-        finish(PIECES - 1, bank_of[PIECES - 1])
+            hid_t = hidden_layer(k, 0, scale_t, shift_t)
+            hid_v = hidden_layer(k, ROWS_EACH, scale_v, shift_v)
+            finish(k, mix(hid_t, hid_v))

@@ -17,9 +17,9 @@ ROWS_EACH = N // ROW
 ROWS = 2 * ROWS_EACH
 PARTS = 3
 PIECE = 256
-PIECES = N // PIECE
-ROWS_IN_PIECE = PIECE // ROW
-LIST_COLUMNS = PIECE // 16
+WIDTHS = [PIECE] * (N // PIECE - 1) + [PIECE // 2] * 2
+PIECES = len(WIDTHS)
+LIST_COLUMN = 16
 
 FLOPS = 2 * 2 * P * P * N
 
@@ -89,10 +89,10 @@ def tile_stratsoriginal_kernel(
         nc.vector.tensor_tensor(words[: 2 * ROWS, :], words[: 2 * ROWS, :], upper(2 * ROWS), SUBTRACT)
         nc.vector.tensor_tensor(words[:ROWS, :], words[:ROWS, :], upper(ROWS), SUBTRACT)
 
-        def hidden_layer(k, first_row, scale, shift):
+        def hidden_layer(start, width, first_row, scale, shift):
             everywhere = spread.tile([P, PIECE], F32, name="everywhere")
-            for i in range(ROWS_IN_PIECE):
-                r = first_row + k * ROWS_IN_PIECE + i
+            for i in range(width // ROW):
+                r = first_row + start // ROW + i
                 nc.tensor.matmul(
                     everywhere[:, i * ROW : (i + 1) * ROW],
                     pick[:, r : r + 1].to_broadcast([P, P]),
@@ -101,25 +101,31 @@ def tile_stratsoriginal_kernel(
                     stop=True,
                 )
             hid = hidden.tile([P, PIECE], BF16, name="hid")
-            nc.scalar.activation(hid[:], everywhere[:], TANH, bias=shift[:], scale=scale[:])
-            return hid
+            nc.scalar.activation(
+                hid[:, :width], everywhere[:, :width], TANH, bias=shift[:], scale=scale[:]
+            )
+            return hid[:, :width]
 
-        def mix(hid_t, hid_v):
+        def mix(width, hid_t, hid_v):
             bank = banks.tile([P, PIECE], F32, name="bank")
-            nc.tensor.matmul(bank[:], mix_t[:], hid_t[:], start=True, stop=False)
-            nc.tensor.matmul(bank[:], mix_v[:], hid_v[:], start=False, stop=True)
-            return bank
+            nc.tensor.matmul(bank[:, :width], mix_t[:], hid_t, start=True, stop=False)
+            nc.tensor.matmul(bank[:, :width], mix_v[:], hid_v, start=False, stop=True)
+            return bank[:, :width]
 
-        def finish(k, bank):
+        def finish(start, width, bank):
             both = result.tile([P, PIECE], F32, name="both")
-            nc.scalar.activation(both[:], bank[:], COPY)
+            nc.scalar.activation(both[:, :width], bank, COPY)
 
-            picked = table[:].indirect(offsets[:, k * LIST_COLUMNS : (k + 1) * LIST_COLUMNS])
+            picked = table[:].indirect(
+                offsets[:, start // LIST_COLUMN : (start + width) // LIST_COLUMN]
+            )
             summed = stored.tile([P, PIECE], F32, name="summed")
-            nc.vector.tensor_tensor(summed[:], picked, both[:], ADD)
-            nc.sync.dma_start(out[:, k * PIECE : (k + 1) * PIECE], summed[:])
+            nc.vector.tensor_tensor(summed[:, :width], picked, both[:, :width], ADD)
+            nc.sync.dma_start(out[:, start : start + width], summed[:, :width])
 
-        for k in range(PIECES):
-            hid_t = hidden_layer(k, 0, scale_t, shift_t)
-            hid_v = hidden_layer(k, ROWS_EACH, scale_v, shift_v)
-            finish(k, mix(hid_t, hid_v))
+        start = 0
+        for width in WIDTHS:
+            hid_t = hidden_layer(start, width, 0, scale_t, shift_t)
+            hid_v = hidden_layer(start, width, ROWS_EACH, scale_v, shift_v)
+            finish(start, width, mix(width, hid_t, hid_v))
+            start += width

@@ -53,7 +53,7 @@ def tile_stratsoriginal_kernel(
                 words[first : first + ROWS_EACH, :],
                 times.rearrange("o (r c) -> (o r) c", c=ROW),
             )
-            nc.sync.dma_start(
+            nc.scalar.dma_start(
                 words[first + ROWS_EACH : first + ROWS, :],
                 values.rearrange("o (r c) -> (o r) c", c=ROW),
             )

@@ -12,12 +12,12 @@ NOT_EQUAL = mybir.AluOpType.not_equal
 P = 128
 S = 1024
 N = 2048
-ROW = 128
-ROWS_EACH = N // ROW
-ROWS = 2 * ROWS_EACH
+ROW = 64
+ROWS = N // ROW
 PARTS = 3
+COPIES = P // ROWS
 PIECE = 256
-WIDTHS = [PIECE] * (N // PIECE - 1) + [PIECE // 2] * 2
+WIDTHS = [PIECE // 2] + [PIECE] * (N // PIECE - 1) + [PIECE // 2]
 PIECES = len(WIDTHS)
 LIST_COLUMN = 16
 
@@ -30,13 +30,13 @@ def tile_stratsoriginal_kernel(
     nc = tc.nc
     with (
         tc.tile_pool(name="held", bufs=1) as held,
-        tc.tile_pool(name="hidden", bufs=2 * PIECES) as hidden,
+        tc.tile_pool(name="hidden", bufs=PIECES) as hidden,
         tc.tile_pool(name="result", bufs=PIECES) as result,
         tc.tile_pool(name="stored", bufs=PIECES) as stored,
-        tc.psum_pool(name="spread", bufs=4) as spread,
+        tc.psum_pool(name="spread", bufs=3) as spread,
         tc.psum_pool(name="banks", bufs=4) as banks,
     ):
-        offsets = held.tile([P, N // 16], U16, name="offsets")
+        offsets = held.tile([P, N // LIST_COLUMN], U16, name="offsets")
         scale_t = held.tile([P, 1], F32, name="scale_t")
         shift_t = held.tile([P, 1], F32, name="shift_t")
         scale_v = held.tile([P, 1], F32, name="scale_v")
@@ -44,26 +44,21 @@ def tile_stratsoriginal_kernel(
         mix_t = held.tile([P, P], BF16, name="mix_t")
         mix_v = held.tile([P, P], BF16, name="mix_v")
         table = held.tile([P, S], F32, name="table")
-        words = held.tile([P, ROW], F32, name="words")
+        words = held.tile([P, 2 * ROW], F32, name="words")
         pick = held.tile([P, ROWS], BF16, name="pick")
 
-        for part in range(PARTS):
-            first = part * ROWS
-            nc.sync.dma_start(
-                words[first : first + ROWS_EACH, :],
-                times.rearrange("o (r c) -> (o r) c", c=ROW),
-            )
-            nc.scalar.dma_start(
-                words[first + ROWS_EACH : first + ROWS, :],
-                values.rearrange("o (r c) -> (o r) c", c=ROW),
-            )
+        def four_times(numbers):
+            return numbers.rearrange("o (r c) -> o r c", c=ROW).to_broadcast([COPIES, ROWS, ROW])
+
+        nc.sync.dma_start(words[:, :ROW], four_times(times))
+        nc.scalar.dma_start(words[:, ROW:], four_times(values))
+        nc.gpsimd.dma_start(table[:], var_table)
         nc.sync.dma_start(scale_t[:], w1t)
         nc.sync.dma_start(shift_t[:], b1t)
         nc.sync.dma_start(scale_v[:], w1v)
         nc.sync.dma_start(shift_v[:], b1v)
         nc.sync.dma_start(mix_t[:], w2t)
         nc.sync.dma_start(mix_v[:], w2v)
-        nc.sync.dma_start(table[:], var_table)
         nc.sync.dma_start(offsets[:], offs)
 
         scratch = held.tile([P, 1], F32, name="scratch")
@@ -85,26 +80,28 @@ def tile_stratsoriginal_kernel(
         def upper(rows):
             return words[:rows, :].bitcast(BF16)[:, 1::2]
 
-        nc.vector.memset(words[PARTS * ROWS :, :], 0.0)
         nc.vector.tensor_tensor(words[: 2 * ROWS, :], words[: 2 * ROWS, :], upper(2 * ROWS), SUBTRACT)
         nc.vector.tensor_tensor(words[:ROWS, :], words[:ROWS, :], upper(ROWS), SUBTRACT)
 
-        def hidden_layer(start, width, first_row, scale, shift):
-            everywhere = spread.tile([P, PIECE], F32, name="everywhere")
+        def spread_numbers(start, width):
+            everywhere = spread.tile([P, PIECE // ROW, 2, ROW], F32, name="everywhere")
             for i in range(width // ROW):
-                r = first_row + start // ROW + i
+                r = start // ROW + i
                 nc.tensor.matmul(
-                    everywhere[:, i * ROW : (i + 1) * ROW],
+                    everywhere[:, i],
                     pick[:, r : r + 1].to_broadcast([P, P]),
                     upper(P),
                     start=True,
                     stop=True,
                 )
-            hid = hidden.tile([P, PIECE], BF16, name="hid")
+            return everywhere[:, : width // ROW]
+
+        def hidden_layer(width, numbers, scale, shift, name):
+            hid = hidden.tile([P, PIECE // ROW, ROW], BF16, name=name)
             nc.scalar.activation(
-                hid[:, :width], everywhere[:, :width], TANH, bias=shift[:], scale=scale[:]
+                hid[:, : width // ROW], numbers, TANH, bias=shift[:], scale=scale[:]
             )
-            return hid[:, :width]
+            return hid[:, : width // ROW].rearrange("p r c -> p (r c)")
 
         def mix(width, hid_t, hid_v):
             bank = banks.tile([P, PIECE], F32, name="bank")
@@ -114,7 +111,10 @@ def tile_stratsoriginal_kernel(
 
         def finish(start, width, bank):
             both = result.tile([P, PIECE], F32, name="both")
-            nc.scalar.activation(both[:, :width], bank, COPY)
+            if start < 2 * PIECE:
+                nc.vector.tensor_copy(both[:, :width], bank)
+            else:
+                nc.scalar.activation(both[:, :width], bank, COPY)
 
             picked = table[:].indirect(
                 offsets[:, start // LIST_COLUMN : (start + width) // LIST_COLUMN]
@@ -125,7 +125,8 @@ def tile_stratsoriginal_kernel(
 
         start = 0
         for width in WIDTHS:
-            hid_t = hidden_layer(start, width, 0, scale_t, shift_t)
-            hid_v = hidden_layer(start, width, ROWS_EACH, scale_v, shift_v)
+            numbers = spread_numbers(start, width)
+            hid_t = hidden_layer(width, numbers[:, :, 0, :], scale_t, shift_t, "hid_t")
+            hid_v = hidden_layer(width, numbers[:, :, 1, :], scale_v, shift_v, "hid_v")
             finish(start, width, mix(width, hid_t, hid_v))
             start += width

@@ -1,4 +1,5 @@
 import concourse.mybir as mybir
+from concourse.masks import make_identity
 
 F32 = mybir.dt.float32
 BF16 = mybir.dt.bfloat16
@@ -6,8 +7,10 @@ U16 = mybir.dt.uint16
 TANH = mybir.ActivationFunctionType.Tanh
 COPY = mybir.ActivationFunctionType.Copy
 ADD = mybir.AluOpType.add
+MULT = mybir.AluOpType.mult
 SUBTRACT = mybir.AluOpType.subtract
-NOT_EQUAL = mybir.AluOpType.not_equal
+MAX = mybir.AluOpType.max
+AXES = mybir.AxisListType
 
 P = 128
 S = 1024
@@ -48,16 +51,16 @@ def tile_stratsoriginal_kernel(
         pick = held.tile([P, ROWS], BF16, name="pick")
 
         def four_times(numbers):
-            return numbers.rearrange("o (r c) -> o r c", c=ROW).to_broadcast([COPIES, ROWS, ROW])
+            return numbers.rearrange("o (r c) -> r o c", c=ROW).to_broadcast([ROWS, COPIES, ROW])
 
         nc.sync.dma_start(words[:, :ROW], four_times(times))
         nc.scalar.dma_start(words[:, ROW:], four_times(values))
-        nc.gpsimd.dma_start(table[:], var_table)
         nc.sync.dma_start(scale_t[:], w1t)
         nc.sync.dma_start(shift_t[:], b1t)
         nc.sync.dma_start(scale_v[:], w1v)
         nc.sync.dma_start(shift_v[:], b1v)
         nc.sync.dma_start(mix_t[:], w2t)
+        nc.sync.dma_start(table[:], var_table)
         nc.sync.dma_start(mix_v[:], w2v)
         nc.sync.dma_start(offsets[:], offs)
 
@@ -65,23 +68,17 @@ def tile_stratsoriginal_kernel(
         nc.vector.memset(scratch[:], 0.0)
         nc.scalar.activation(scratch[:], scratch[:], TANH)
 
-        nc.gpsimd.memset(pick[:], 0.0)
-        for part in range(PARTS):
-            nc.gpsimd.affine_select(
-                out=pick[:],
-                in_=pick[:],
-                compare_op=NOT_EQUAL,
-                fill=1.0,
-                base=-part * ROWS,
-                pattern=[[-1, ROWS]],
-                channel_multiplier=1,
-            )
+        identity = held.tile([P, ROWS, COPIES], BF16, name="identity")
+        make_identity(nc, identity[:].rearrange("k r c -> k (r c)"))
+        once = held.tile([P, 1], F32, name="once")
+        twice = held.tile([P, 1], F32, name="twice")
+        nc.vector.tensor_reduce(once[:], identity[:, :, 1:], AXES.XY, MAX)
+        nc.vector.tensor_reduce(twice[:], identity[:, :, 2:], AXES.XY, MAX)
+        nc.vector.tensor_reduce(pick[:], identity[:, :, :PARTS], AXES.X, MAX)
 
-        def upper(rows):
-            return words[:rows, :].bitcast(BF16)[:, 1::2]
-
-        nc.vector.tensor_tensor(words[: 2 * ROWS, :], words[: 2 * ROWS, :], upper(2 * ROWS), SUBTRACT)
-        nc.vector.tensor_tensor(words[:ROWS, :], words[:ROWS, :], upper(ROWS), SUBTRACT)
+        upper = words[:].bitcast(BF16)[:, 1::2]
+        for factor in (once, twice):
+            nc.vector.scalar_tensor_tensor(words[:], upper, factor[:], words[:], MULT, SUBTRACT)
 
         def spread_numbers(start, width):
             everywhere = spread.tile([P, PIECE // ROW, 2, ROW], F32, name="everywhere")
@@ -90,7 +87,7 @@ def tile_stratsoriginal_kernel(
                 nc.tensor.matmul(
                     everywhere[:, i],
                     pick[:, r : r + 1].to_broadcast([P, P]),
-                    upper(P),
+                    upper,
                     start=True,
                     stop=True,
                 )

@@ -1,5 +1,4 @@
 import concourse.mybir as mybir
-from concourse.masks import make_identity
 
 F32 = mybir.dt.float32
 BF16 = mybir.dt.bfloat16
@@ -9,18 +8,16 @@ COPY = mybir.ActivationFunctionType.Copy
 ADD = mybir.AluOpType.add
 MULT = mybir.AluOpType.mult
 SUBTRACT = mybir.AluOpType.subtract
-MAX = mybir.AluOpType.max
-AXES = mybir.AxisListType
+NOT_EQUAL = mybir.AluOpType.not_equal
 
 P = 128
 S = 1024
 N = 2048
-ROW = 64
-ROWS = N // ROW
-PARTS = 3
-COPIES = P // ROWS
 PIECE = 256
-WIDTHS = [PIECE // 2] + [PIECE] * (N // PIECE - 1) + [PIECE // 2]
+ROWS = N // PIECE
+COPIES = P // ROWS
+QUARTER = P // 4
+WIDTHS = [PIECE] * (ROWS - 1) + [PIECE // 2] * 2
 PIECES = len(WIDTHS)
 LIST_COLUMN = 16
 
@@ -33,10 +30,10 @@ def tile_stratsoriginal_kernel(
     nc = tc.nc
     with (
         tc.tile_pool(name="held", bufs=1) as held,
-        tc.tile_pool(name="hidden", bufs=PIECES) as hidden,
+        tc.tile_pool(name="hidden", bufs=2 * PIECES) as hidden,
         tc.tile_pool(name="result", bufs=PIECES) as result,
         tc.tile_pool(name="stored", bufs=PIECES) as stored,
-        tc.psum_pool(name="spread", bufs=3) as spread,
+        tc.psum_pool(name="spread", bufs=4) as spread,
         tc.psum_pool(name="banks", bufs=4) as banks,
     ):
         offsets = held.tile([P, N // LIST_COLUMN], U16, name="offsets")
@@ -47,14 +44,17 @@ def tile_stratsoriginal_kernel(
         mix_t = held.tile([P, P], BF16, name="mix_t")
         mix_v = held.tile([P, P], BF16, name="mix_v")
         table = held.tile([P, S], F32, name="table")
-        words = held.tile([P, 2 * ROW], F32, name="words")
-        pick = held.tile([P, ROWS], BF16, name="pick")
+        words_t = held.tile([P, PIECE], F32, name="words_t")
+        words_v = held.tile([P, PIECE], F32, name="words_v")
+        rest_t = held.tile([P, PIECE], F32, name="rest_t")
+        rest_v = held.tile([P, PIECE], F32, name="rest_v")
 
-        def four_times(numbers):
-            return numbers.rearrange("o (r c) -> r o c", c=ROW).to_broadcast([ROWS, COPIES, ROW])
+        def sixteen_times(numbers):
+            rows = numbers.rearrange("o (r c) -> o r c", c=PIECE)
+            return rows.to_broadcast([COPIES, ROWS, PIECE])
 
-        nc.sync.dma_start(words[:, :ROW], four_times(times))
-        nc.scalar.dma_start(words[:, ROW:], four_times(values))
+        nc.sync.dma_start(words_t[:], sixteen_times(times))
+        nc.scalar.dma_start(words_v[:], sixteen_times(values))
         nc.sync.dma_start(scale_t[:], w1t)
         nc.sync.dma_start(shift_t[:], b1t)
         nc.sync.dma_start(scale_v[:], w1v)
@@ -68,50 +68,70 @@ def tile_stratsoriginal_kernel(
         nc.vector.memset(scratch[:], 0.0)
         nc.scalar.activation(scratch[:], scratch[:], TANH)
 
-        identity = held.tile([P, ROWS, COPIES], BF16, name="identity")
-        make_identity(nc, identity[:].rearrange("k r c -> k (r c)"))
+        pick_high = held.tile([P, ROWS], BF16, name="pick_high")
+        pick_rest = held.tile([P, ROWS], BF16, name="pick_rest")
+        pick = held.tile([P, ROWS], BF16, name="pick")
+        for weights, quarters in ((pick_high, (2,)), (pick_rest, (0, 1))):
+            nc.gpsimd.memset(weights[:], 0.0)
+            for quarter in quarters:
+                nc.gpsimd.affine_select(
+                    out=weights[:],
+                    in_=weights[:],
+                    compare_op=NOT_EQUAL,
+                    fill=1.0,
+                    base=-quarter * QUARTER,
+                    pattern=[[-1, ROWS]],
+                    channel_multiplier=1,
+                )
+        nc.vector.tensor_tensor(pick[:], pick_high[:], pick_rest[:], ADD)
+
         once = held.tile([P, 1], F32, name="once")
         twice = held.tile([P, 1], F32, name="twice")
-        nc.vector.tensor_reduce(once[:], identity[:, :, 1:], AXES.XY, MAX)
-        nc.vector.tensor_reduce(twice[:], identity[:, :, 2:], AXES.XY, MAX)
-        nc.vector.tensor_reduce(pick[:], identity[:, :, :PARTS], AXES.X, MAX)
+        nc.vector.memset(once[: 2 * QUARTER], 1.0)
+        nc.vector.memset(once[2 * QUARTER :], 0.0)
+        nc.vector.memset(twice[:], 0.0)
+        nc.vector.memset(twice[:QUARTER], 1.0)
 
-        upper = words[:].bitcast(BF16)[:, 1::2]
-        for factor in (once, twice):
-            nc.vector.scalar_tensor_tensor(words[:], upper, factor[:], words[:], MULT, SUBTRACT)
+        def upper(words):
+            return words[:].bitcast(BF16)[:, 1::2]
 
-        def spread_numbers(start, width):
-            everywhere = spread.tile([P, PIECE // ROW, 2, ROW], F32, name="everywhere")
-            for i in range(width // ROW):
-                r = start // ROW + i
-                nc.tensor.matmul(
-                    everywhere[:, i],
-                    pick[:, r : r + 1].to_broadcast([P, P]),
-                    upper,
-                    start=True,
-                    stop=True,
-                )
-            return everywhere[:, : width // ROW]
+        for words, rest in ((words_t, rest_t), (words_v, rest_v)):
+            nc.vector.scalar_tensor_tensor(rest[:], upper(words), once[:], words[:], MULT, SUBTRACT)
+            nc.vector.scalar_tensor_tensor(rest[:], upper(rest), twice[:], rest[:], MULT, SUBTRACT)
 
-        def hidden_layer(width, numbers, scale, shift, name):
-            hid = hidden.tile([P, PIECE // ROW, ROW], BF16, name=name)
-            nc.scalar.activation(
-                hid[:, : width // ROW], numbers, TANH, bias=shift[:], scale=scale[:]
-            )
-            return hid[:, : width // ROW].rearrange("p r c -> p (r c)")
+        def ones(weights, row):
+            return weights[:, row : row + 1].to_broadcast([P, P])
 
-        def mix(width, hid_t, hid_v):
+        def spread_high(row, words):
+            everywhere = spread.tile([P, PIECE], F32, name="everywhere")
+            nc.tensor.matmul(everywhere[:], ones(pick_high, row), upper(words), start=True, stop=False)
+            return everywhere
+
+        def hidden_layer(start, width, opened, rest, scale, shift):
+            row, first = start // PIECE, start % PIECE
+            parts = upper(rest)[:, first : first + width]
+            if row in opened:
+                everywhere = opened[row]
+                numbers = everywhere[:, :width]
+                nc.tensor.matmul(numbers, ones(pick_rest, row), parts, start=False, stop=True)
+            else:
+                everywhere = spread.tile([P, PIECE], F32, name="everywhere")
+                numbers = everywhere[:, :width]
+                nc.tensor.matmul(numbers, ones(pick, row), parts, start=True, stop=True)
+            hid = hidden.tile([P, PIECE], BF16, name="hid")
+            nc.scalar.activation(hid[:, :width], numbers, TANH, bias=shift[:], scale=scale[:])
+            return hid[:, :width]
+
+        def finish(start, width, hid_t, hid_v):
             bank = banks.tile([P, PIECE], F32, name="bank")
             nc.tensor.matmul(bank[:, :width], mix_t[:], hid_t, start=True, stop=False)
             nc.tensor.matmul(bank[:, :width], mix_v[:], hid_v, start=False, stop=True)
-            return bank[:, :width]
 
-        def finish(start, width, bank):
             both = result.tile([P, PIECE], F32, name="both")
-            if start < 2 * PIECE:
-                nc.vector.tensor_copy(both[:, :width], bank)
+            if start < N // 3:
+                nc.vector.tensor_copy(both[:, :width], bank[:, :width])
             else:
-                nc.scalar.activation(both[:, :width], bank, COPY)
+                nc.scalar.activation(both[:, :width], bank[:, :width], COPY)
 
             picked = table[:].indirect(
                 offsets[:, start // LIST_COLUMN : (start + width) // LIST_COLUMN]
@@ -120,10 +140,18 @@ def tile_stratsoriginal_kernel(
             nc.vector.tensor_tensor(summed[:, :width], picked, both[:, :width], ADD)
             nc.sync.dma_start(out[:, start : start + width], summed[:, :width])
 
+        opened_t, opened_v = {}, {}
+        for row in range(2):
+            opened_t[row] = spread_high(row, words_t)
+            opened_v[row] = spread_high(row, words_v)
+
         start = 0
+        waiting = []
         for width in WIDTHS:
-            numbers = spread_numbers(start, width)
-            hid_t = hidden_layer(width, numbers[:, :, 0, :], scale_t, shift_t, "hid_t")
-            hid_v = hidden_layer(width, numbers[:, :, 1, :], scale_v, shift_v, "hid_v")
-            finish(start, width, mix(width, hid_t, hid_v))
+            hid_t = hidden_layer(start, width, opened_t, rest_t, scale_t, shift_t)
+            hid_v = hidden_layer(start, width, opened_v, rest_v, scale_v, shift_v)
+            for piece in waiting:
+                finish(*piece)
+            waiting = [(start, width, hid_t, hid_v)]
             start += width
+        finish(*waiting[0])

@@ -60,9 +60,9 @@ def tile_stratsoriginal_kernel(
         nc.sync.dma_start(scale_v[:], w1v)
         nc.sync.dma_start(shift_v[:], b1v)
         nc.sync.dma_start(mix_t[:], w2t)
-        nc.sync.dma_start(table[:], var_table)
         nc.sync.dma_start(mix_v[:], w2v)
         nc.sync.dma_start(offsets[:], offs)
+        nc.sync.dma_start(table[:], var_table)
 
         scratch = held.tile([P, 1], F32, name="scratch")
         nc.vector.memset(scratch[:], 0.0)
@@ -146,12 +146,8 @@ def tile_stratsoriginal_kernel(
             opened_v[row] = spread_high(row, words_v)
 
         start = 0
-        waiting = []
         for width in WIDTHS:
             hid_t = hidden_layer(start, width, opened_t, rest_t, scale_t, shift_t)
             hid_v = hidden_layer(start, width, opened_v, rest_v, scale_v, shift_v)
-            for piece in waiting:
-                finish(*piece)
-            waiting = [(start, width, hid_t, hid_v)]
+            finish(start, width, hid_t, hid_v)
             start += width
-        finish(*waiting[0])

@@ -13,11 +13,12 @@ NOT_EQUAL = mybir.AluOpType.not_equal
 P = 128
 S = 1024
 N = 2048
-PIECE = 256
-ROWS = N // PIECE
+ROW = 128
+ROWS = N // ROW
 COPIES = P // ROWS
 QUARTER = P // 4
-WIDTHS = [PIECE] * (ROWS - 1) + [PIECE // 2] * 2
+PIECE = 256
+WIDTHS = [PIECE // 2] * 2 + [PIECE] * (N // PIECE - 2) + [PIECE // 2] * 2
 PIECES = len(WIDTHS)
 LIST_COLUMN = 16
 
@@ -33,8 +34,8 @@ def tile_stratsoriginal_kernel(
         tc.tile_pool(name="hidden", bufs=2 * PIECES) as hidden,
         tc.tile_pool(name="result", bufs=PIECES) as result,
         tc.tile_pool(name="stored", bufs=PIECES) as stored,
-        tc.psum_pool(name="spread", bufs=4) as spread,
-        tc.psum_pool(name="banks", bufs=4) as banks,
+        tc.psum_pool(name="spread", bufs=5) as spread,
+        tc.psum_pool(name="banks", bufs=3) as banks,
     ):
         offsets = held.tile([P, N // LIST_COLUMN], U16, name="offsets")
         scale_t = held.tile([P, 1], F32, name="scale_t")
@@ -44,25 +45,25 @@ def tile_stratsoriginal_kernel(
         mix_t = held.tile([P, P], BF16, name="mix_t")
         mix_v = held.tile([P, P], BF16, name="mix_v")
         table = held.tile([P, S], F32, name="table")
-        words_t = held.tile([P, PIECE], F32, name="words_t")
-        words_v = held.tile([P, PIECE], F32, name="words_v")
-        rest_t = held.tile([P, PIECE], F32, name="rest_t")
-        rest_v = held.tile([P, PIECE], F32, name="rest_v")
+        words_t = held.tile([P, ROW], F32, name="words_t")
+        words_v = held.tile([P, ROW], F32, name="words_v")
+        rest_t = held.tile([P, ROW], F32, name="rest_t")
+        rest_v = held.tile([P, ROW], F32, name="rest_v")
 
-        def sixteen_times(numbers):
-            rows = numbers.rearrange("o (r c) -> o r c", c=PIECE)
-            return rows.to_broadcast([COPIES, ROWS, PIECE])
+        def eight_times(numbers):
+            rows = numbers.rearrange("o (r c) -> o r c", c=ROW)
+            return rows.to_broadcast([COPIES, ROWS, ROW])
 
-        nc.sync.dma_start(words_t[:], sixteen_times(times))
-        nc.scalar.dma_start(words_v[:], sixteen_times(values))
+        nc.sync.dma_start(words_t[:], eight_times(times))
+        nc.scalar.dma_start(words_v[:], eight_times(values))
         nc.sync.dma_start(scale_t[:], w1t)
         nc.sync.dma_start(shift_t[:], b1t)
         nc.sync.dma_start(scale_v[:], w1v)
         nc.sync.dma_start(shift_v[:], b1v)
         nc.sync.dma_start(mix_t[:], w2t)
+        nc.sync.dma_start(table[:], var_table)
         nc.sync.dma_start(mix_v[:], w2v)
         nc.sync.dma_start(offsets[:], offs)
-        nc.sync.dma_start(table[:], var_table)
 
         scratch = held.tile([P, 1], F32, name="scratch")
         nc.vector.memset(scratch[:], 0.0)
@@ -104,22 +105,26 @@ def tile_stratsoriginal_kernel(
 
         def spread_high(row, words):
             everywhere = spread.tile([P, PIECE], F32, name="everywhere")
-            nc.tensor.matmul(everywhere[:], ones(pick_high, row), upper(words), start=True, stop=False)
+            numbers = everywhere[:, :ROW]
+            nc.tensor.matmul(numbers, ones(pick_high, row), upper(words), start=True, stop=False)
             return everywhere
 
         def hidden_layer(start, width, opened, rest, scale, shift):
-            row, first = start // PIECE, start % PIECE
-            parts = upper(rest)[:, first : first + width]
-            if row in opened:
-                everywhere = opened[row]
-                numbers = everywhere[:, :width]
-                nc.tensor.matmul(numbers, ones(pick_rest, row), parts, start=False, stop=True)
+            rows = range(start // ROW, (start + width) // ROW)
+            if rows[0] in opened:
+                everywhere = opened[rows[0]]
             else:
                 everywhere = spread.tile([P, PIECE], F32, name="everywhere")
-                numbers = everywhere[:, :width]
-                nc.tensor.matmul(numbers, ones(pick, row), parts, start=True, stop=True)
+            for i, row in enumerate(rows):
+                numbers = everywhere[:, i * ROW : (i + 1) * ROW]
+                if row in opened:
+                    nc.tensor.matmul(numbers, ones(pick_rest, row), upper(rest), start=False, stop=True)
+                else:
+                    nc.tensor.matmul(numbers, ones(pick, row), upper(rest), start=True, stop=True)
             hid = hidden.tile([P, PIECE], BF16, name="hid")
-            nc.scalar.activation(hid[:, :width], numbers, TANH, bias=shift[:], scale=scale[:])
+            nc.scalar.activation(
+                hid[:, :width], everywhere[:, :width], TANH, bias=shift[:], scale=scale[:]
+            )
             return hid[:, :width]
 
         def finish(start, width, hid_t, hid_v):
@@ -128,7 +133,7 @@ def tile_stratsoriginal_kernel(
             nc.tensor.matmul(bank[:, :width], mix_v[:], hid_v, start=False, stop=True)
 
             both = result.tile([P, PIECE], F32, name="both")
-            if start < N // 3:
+            if start < N // 4:
                 nc.vector.tensor_copy(both[:, :width], bank[:, :width])
             else:
                 nc.scalar.activation(both[:, :width], bank[:, :width], COPY)
@@ -144,6 +149,7 @@ def tile_stratsoriginal_kernel(
         for row in range(2):
             opened_t[row] = spread_high(row, words_t)
             opened_v[row] = spread_high(row, words_v)
+        opened_t[2] = spread_high(2, words_t)
 
         start = 0
         for width in WIDTHS:

@@ -1,4 +1,5 @@
 import concourse.mybir as mybir
+from concourse.masks import make_identity
 
 F32 = mybir.dt.float32
 BF16 = mybir.dt.bfloat16
@@ -8,7 +9,8 @@ COPY = mybir.ActivationFunctionType.Copy
 ADD = mybir.AluOpType.add
 MULT = mybir.AluOpType.mult
 SUBTRACT = mybir.AluOpType.subtract
-NOT_EQUAL = mybir.AluOpType.not_equal
+MAX = mybir.AluOpType.max
+AXES = mybir.AxisListType
 
 P = 128
 S = 1024
@@ -16,7 +18,7 @@ N = 2048
 ROW = 128
 ROWS = N // ROW
 COPIES = P // ROWS
-QUARTER = P // 4
+PARTS = 3
 PIECE = 256
 WIDTHS = [PIECE // 2] * 2 + [PIECE] * (N // PIECE - 2) + [PIECE // 2] * 2
 PIECES = len(WIDTHS)
@@ -51,8 +53,7 @@ def tile_stratsoriginal_kernel(
         rest_v = held.tile([P, ROW], F32, name="rest_v")
 
         def eight_times(numbers):
-            rows = numbers.rearrange("o (r c) -> o r c", c=ROW)
-            return rows.to_broadcast([COPIES, ROWS, ROW])
+            return numbers.rearrange("o (r c) -> r o c", c=ROW).to_broadcast([ROWS, COPIES, ROW])
 
         nc.sync.dma_start(words_t[:], eight_times(times))
         nc.scalar.dma_start(words_v[:], eight_times(values))
@@ -69,29 +70,17 @@ def tile_stratsoriginal_kernel(
         nc.vector.memset(scratch[:], 0.0)
         nc.scalar.activation(scratch[:], scratch[:], TANH)
 
-        pick_high = held.tile([P, ROWS], BF16, name="pick_high")
-        pick_rest = held.tile([P, ROWS], BF16, name="pick_rest")
-        pick = held.tile([P, ROWS], BF16, name="pick")
-        for weights, quarters in ((pick_high, (2,)), (pick_rest, (0, 1))):
-            nc.gpsimd.memset(weights[:], 0.0)
-            for quarter in quarters:
-                nc.gpsimd.affine_select(
-                    out=weights[:],
-                    in_=weights[:],
-                    compare_op=NOT_EQUAL,
-                    fill=1.0,
-                    base=-quarter * QUARTER,
-                    pattern=[[-1, ROWS]],
-                    channel_multiplier=1,
-                )
-        nc.vector.tensor_tensor(pick[:], pick_high[:], pick_rest[:], ADD)
-
+        identity = held.tile([P, ROWS, COPIES], BF16, name="identity")
+        make_identity(nc, identity[:].rearrange("k r c -> k (r c)"))
         once = held.tile([P, 1], F32, name="once")
         twice = held.tile([P, 1], F32, name="twice")
-        nc.vector.memset(once[: 2 * QUARTER], 1.0)
-        nc.vector.memset(once[2 * QUARTER :], 0.0)
-        nc.vector.memset(twice[:], 0.0)
-        nc.vector.memset(twice[:QUARTER], 1.0)
+        pick_rest = held.tile([P, ROWS], BF16, name="pick_rest")
+        pick = held.tile([P, ROWS], BF16, name="pick")
+        pick_high = identity[:, :, 0]
+        nc.vector.tensor_reduce(once[:], identity[:, :, 1:], AXES.XY, MAX)
+        nc.vector.tensor_reduce(twice[:], identity[:, :, 2:], AXES.XY, MAX)
+        nc.vector.tensor_reduce(pick_rest[:], identity[:, :, 1:PARTS], AXES.X, MAX)
+        nc.vector.tensor_reduce(pick[:], identity[:, :, :PARTS], AXES.X, MAX)
 
         def upper(words):
             return words[:].bitcast(BF16)[:, 1::2]

@@ -20,7 +20,7 @@ ROWS = N // ROW
 COPIES = P // ROWS
 PARTS = 3
 PIECE = 256
-WIDTHS = [PIECE // 2] * 2 + [PIECE] * (N // PIECE - 2) + [PIECE // 2] * 2
+WIDTHS = [PIECE] * (N // PIECE - 1) + [PIECE // 2] * 2
 PIECES = len(WIDTHS)
 LIST_COLUMN = 16
 
@@ -36,8 +36,8 @@ def tile_stratsoriginal_kernel(
         tc.tile_pool(name="hidden", bufs=2 * PIECES) as hidden,
         tc.tile_pool(name="result", bufs=PIECES) as result,
         tc.tile_pool(name="stored", bufs=PIECES) as stored,
-        tc.psum_pool(name="spread", bufs=5) as spread,
-        tc.psum_pool(name="banks", bufs=3) as banks,
+        tc.psum_pool(name="spread", bufs=4) as spread,
+        tc.psum_pool(name="banks", bufs=4) as banks,
     ):
         offsets = held.tile([P, N // LIST_COLUMN], U16, name="offsets")
         scale_t = held.tile([P, 1], F32, name="scale_t")
@@ -49,8 +49,6 @@ def tile_stratsoriginal_kernel(
         table = held.tile([P, S], F32, name="table")
         words_t = held.tile([P, ROW], F32, name="words_t")
         words_v = held.tile([P, ROW], F32, name="words_v")
-        rest_t = held.tile([P, ROW], F32, name="rest_t")
-        rest_v = held.tile([P, ROW], F32, name="rest_v")
 
         def eight_times(numbers):
             return numbers.rearrange("o (r c) -> r o c", c=ROW).to_broadcast([ROWS, COPIES, ROW])
@@ -74,42 +72,31 @@ def tile_stratsoriginal_kernel(
         make_identity(nc, identity[:].rearrange("k r c -> k (r c)"))
         once = held.tile([P, 1], F32, name="once")
         twice = held.tile([P, 1], F32, name="twice")
-        pick_rest = held.tile([P, ROWS], BF16, name="pick_rest")
         pick = held.tile([P, ROWS], BF16, name="pick")
-        pick_high = identity[:, :, 0]
         nc.vector.tensor_reduce(once[:], identity[:, :, 1:], AXES.XY, MAX)
         nc.vector.tensor_reduce(twice[:], identity[:, :, 2:], AXES.XY, MAX)
-        nc.vector.tensor_reduce(pick_rest[:], identity[:, :, 1:PARTS], AXES.X, MAX)
         nc.vector.tensor_reduce(pick[:], identity[:, :, :PARTS], AXES.X, MAX)
 
         def upper(words):
             return words[:].bitcast(BF16)[:, 1::2]
 
-        for words, rest in ((words_t, rest_t), (words_v, rest_v)):
-            nc.vector.scalar_tensor_tensor(rest[:], upper(words), once[:], words[:], MULT, SUBTRACT)
-            nc.vector.scalar_tensor_tensor(rest[:], upper(rest), twice[:], rest[:], MULT, SUBTRACT)
+        for words in (words_t, words_v):
+            for factor in (once, twice):
+                nc.vector.scalar_tensor_tensor(
+                    words[:], upper(words), factor[:], words[:], MULT, SUBTRACT
+                )
 
-        def ones(weights, row):
-            return weights[:, row : row + 1].to_broadcast([P, P])
-
-        def spread_high(row, words):
+        def hidden_layer(start, width, words, scale, shift):
             everywhere = spread.tile([P, PIECE], F32, name="everywhere")
-            numbers = everywhere[:, :ROW]
-            nc.tensor.matmul(numbers, ones(pick_high, row), upper(words), start=True, stop=False)
-            return everywhere
-
-        def hidden_layer(start, width, opened, rest, scale, shift):
-            rows = range(start // ROW, (start + width) // ROW)
-            if rows[0] in opened:
-                everywhere = opened[rows[0]]
-            else:
-                everywhere = spread.tile([P, PIECE], F32, name="everywhere")
-            for i, row in enumerate(rows):
-                numbers = everywhere[:, i * ROW : (i + 1) * ROW]
-                if row in opened:
-                    nc.tensor.matmul(numbers, ones(pick_rest, row), upper(rest), start=False, stop=True)
-                else:
-                    nc.tensor.matmul(numbers, ones(pick, row), upper(rest), start=True, stop=True)
+            for i in range(width // ROW):
+                row = start // ROW + i
+                nc.tensor.matmul(
+                    everywhere[:, i * ROW : (i + 1) * ROW],
+                    pick[:, row : row + 1].to_broadcast([P, P]),
+                    upper(words),
+                    start=True,
+                    stop=True,
+                )
             hid = hidden.tile([P, PIECE], BF16, name="hid")
             nc.scalar.activation(
                 hid[:, :width], everywhere[:, :width], TANH, bias=shift[:], scale=scale[:]
@@ -122,7 +109,7 @@ def tile_stratsoriginal_kernel(
             nc.tensor.matmul(bank[:, :width], mix_v[:], hid_v, start=False, stop=True)
 
             both = result.tile([P, PIECE], F32, name="both")
-            if start < N // 4:
+            if start < N // 3:
                 nc.vector.tensor_copy(both[:, :width], bank[:, :width])
             else:
                 nc.scalar.activation(both[:, :width], bank[:, :width], COPY)
@@ -134,15 +121,13 @@ def tile_stratsoriginal_kernel(
             nc.vector.tensor_tensor(summed[:, :width], picked, both[:, :width], ADD)
             nc.sync.dma_start(out[:, start : start + width], summed[:, :width])
 
-        opened_t, opened_v = {}, {}
-        for row in range(2):
-            opened_t[row] = spread_high(row, words_t)
-            opened_v[row] = spread_high(row, words_v)
-        opened_t[2] = spread_high(2, words_t)
-
         start = 0
+        waiting = []
         for width in WIDTHS:
-            hid_t = hidden_layer(start, width, opened_t, rest_t, scale_t, shift_t)
-            hid_v = hidden_layer(start, width, opened_v, rest_v, scale_v, shift_v)
-            finish(start, width, hid_t, hid_v)
+            hid_t = hidden_layer(start, width, words_t, scale_t, shift_t)
+            hid_v = hidden_layer(start, width, words_v, scale_v, shift_v)
+            for piece in waiting:
+                finish(*piece)
+            waiting = [(start, width, hid_t, hid_v)]
             start += width
+        finish(*waiting[0])

import concourse.mybir as mybir
from concourse.masks import make_identity

F32 = mybir.dt.float32
BF16 = mybir.dt.bfloat16
U16 = mybir.dt.uint16
TANH = mybir.ActivationFunctionType.Tanh
COPY = mybir.ActivationFunctionType.Copy
ADD = mybir.AluOpType.add
MULT = mybir.AluOpType.mult
SUBTRACT = mybir.AluOpType.subtract
MAX = mybir.AluOpType.max
AXES = mybir.AxisListType

P = 128
S = 1024
N = 2048
ROW = 128
ROWS = N // ROW
COPIES = P // ROWS
PARTS = 3
PIECE = 256
WIDTHS = [PIECE] * (N // PIECE - 1) + [PIECE // 2] * 2
PIECES = len(WIDTHS)
LIST_COLUMN = 16

FLOPS = 2 * 2 * P * P * N


def tile_stratsoriginal_kernel(
    tc, var_table, times, values, w1t, b1t, w2t, w1v, b1v, w2v, offs, out
):
    nc = tc.nc
    with (
        tc.tile_pool(name="held", bufs=1) as held,
        tc.tile_pool(name="hidden", bufs=2 * PIECES) as hidden,
        tc.tile_pool(name="result", bufs=PIECES) as result,
        tc.tile_pool(name="stored", bufs=PIECES) as stored,
        tc.psum_pool(name="spread", bufs=4) as spread,
        tc.psum_pool(name="banks", bufs=4) as banks,
    ):
        offsets = held.tile([P, N // LIST_COLUMN], U16, name="offsets")
        scale_t = held.tile([P, 1], F32, name="scale_t")
        shift_t = held.tile([P, 1], F32, name="shift_t")
        scale_v = held.tile([P, 1], F32, name="scale_v")
        shift_v = held.tile([P, 1], F32, name="shift_v")
        mix_t = held.tile([P, P], BF16, name="mix_t")
        mix_v = held.tile([P, P], BF16, name="mix_v")
        table = held.tile([P, S], F32, name="table")
        words_t = held.tile([P, ROW], F32, name="words_t")
        words_v = held.tile([P, ROW], F32, name="words_v")

        def eight_times(numbers):
            return numbers.rearrange("o (r c) -> r o c", c=ROW).to_broadcast([ROWS, COPIES, ROW])

        nc.sync.dma_start(words_t[:], eight_times(times))
        nc.scalar.dma_start(words_v[:], eight_times(values))
        nc.sync.dma_start(scale_t[:], w1t)
        nc.sync.dma_start(shift_t[:], b1t)
        nc.sync.dma_start(scale_v[:], w1v)
        nc.sync.dma_start(shift_v[:], b1v)
        nc.sync.dma_start(mix_t[:], w2t)
        nc.sync.dma_start(table[:], var_table)
        nc.sync.dma_start(mix_v[:], w2v)
        nc.sync.dma_start(offsets[:], offs)

        scratch = held.tile([P, 1], F32, name="scratch")
        nc.vector.memset(scratch[:], 0.0)
        nc.scalar.activation(scratch[:], scratch[:], TANH)

        identity = held.tile([P, ROWS, COPIES], BF16, name="identity")
        make_identity(nc, identity[:].rearrange("k r c -> k (r c)"))
        once = held.tile([P, 1], F32, name="once")
        twice = held.tile([P, 1], F32, name="twice")
        pick = held.tile([P, ROWS], BF16, name="pick")
        nc.vector.tensor_reduce(once[:], identity[:, :, 1:], AXES.XY, MAX)
        nc.vector.tensor_reduce(twice[:], identity[:, :, 2:], AXES.XY, MAX)
        nc.vector.tensor_reduce(pick[:], identity[:, :, :PARTS], AXES.X, MAX)

        def upper(words):
            return words[:].bitcast(BF16)[:, 1::2]

        for words in (words_t, words_v):
            for factor in (once, twice):
                nc.vector.scalar_tensor_tensor(
                    words[:], upper(words), factor[:], words[:], MULT, SUBTRACT
                )

        def hidden_layer(start, width, words, scale, shift):
            everywhere = spread.tile([P, PIECE], F32, name="everywhere")
            for i in range(width // ROW):
                row = start // ROW + i
                nc.tensor.matmul(
                    everywhere[:, i * ROW : (i + 1) * ROW],
                    pick[:, row : row + 1].to_broadcast([P, P]),
                    upper(words),
                    start=True,
                    stop=True,
                )
            hid = hidden.tile([P, PIECE], BF16, name="hid")
            nc.scalar.activation(
                hid[:, :width], everywhere[:, :width], TANH, bias=shift[:], scale=scale[:]
            )
            return hid[:, :width]

        def finish(start, width, hid_t, hid_v):
            bank = banks.tile([P, PIECE], F32, name="bank")
            nc.tensor.matmul(bank[:, :width], mix_t[:], hid_t, start=True, stop=False)
            nc.tensor.matmul(bank[:, :width], mix_v[:], hid_v, start=False, stop=True)

            both = result.tile([P, PIECE], F32, name="both")
            if start < N // 3:
                nc.vector.tensor_copy(both[:, :width], bank[:, :width])
            else:
                nc.scalar.activation(both[:, :width], bank[:, :width], COPY)

            picked = table[:].indirect(
                offsets[:, start // LIST_COLUMN : (start + width) // LIST_COLUMN]
            )
            summed = stored.tile([P, PIECE], F32, name="summed")
            nc.vector.tensor_tensor(summed[:, :width], picked, both[:, :width], ADD)
            nc.sync.dma_start(out[:, start : start + width], summed[:, :width])

        start = 0
        waiting = []
        for width in WIDTHS:
            hid_t = hidden_layer(start, width, words_t, scale_t, shift_t)
            hid_v = hidden_layer(start, width, words_v, scale_v, shift_v)
            for piece in waiting:
                finish(*piece)
            waiting = [(start, width, hid_t, hid_v)]
            start += width
        finish(*waiting[0])
